import numpy as np
import ml_dtypes


def mxq(x, axis, fmt="e4m3"):
    dtype, down = {"e4m3": (ml_dtypes.float8_e4m3fn, 7), "e5m2": (ml_dtypes.float8_e5m2, 14)}[fmt]
    v = np.moveaxis(np.asarray(x, np.float32).astype(ml_dtypes.bfloat16).astype(np.float64), axis, -1)
    blocks = v.reshape(v.shape[:-1] + (-1, 32))
    amax = np.abs(blocks).max(-1, keepdims=True)
    byte = np.maximum(np.where(amax > 0, np.frexp(amax)[1] - 1 + 127, 0) - down, 1)
    scale = np.exp2(byte - 127.0)
    codes = (blocks / scale).astype(np.float32).astype(dtype).astype(np.float64)
    return np.moveaxis((codes * scale).reshape(v.shape), -1, axis)


WIDE = False


def mx_kscale(k):
    if not WIDE:
        return np.ones(k)
    levels = np.array([10, -10, 5, -5, 0])
    a = np.random.permutation(np.resize(levels, k // 512 * 4)).reshape(k // 512, 4)
    idx = np.arange(k)
    return np.exp2(a[idx // 512, idx % 128 // 32])


BF16 = ml_dtypes.bfloat16


def bf(x):
    return np.asarray(x, np.float32).astype(BF16)


def f64(x):
    return np.asarray(x).astype(np.float64)


E2M1 = np.array([0.0, 0.5, 1.0, 1.5, 2.0, 3.0, 4.0, 6.0, -0.0, -0.5, -1.0, -1.5, -2.0, -3.0, -4.0, -6.0])


def pack_weight(w, fmt):
    k, n = w.shape
    w = f64(bf(w)).reshape(k // 32, 32, n)
    amax = np.abs(w).max(1)
    if fmt == "e4m3":
        byte = np.frexp(amax)[1] - 1 + 127 - 7
    else:
        mant, ex = np.frexp(amax / 6.0)
        byte = np.where(mant > 0.5, ex, ex - 1) + 127
    byte = np.clip(np.where(amax > 0, byte, 1), 1, 254)
    scaled = (w * np.exp2(127.0 - byte)[:, None, :]).reshape(k, n).astype(np.float32)
    by_word = np.ascontiguousarray(scaled.reshape(k // 512, 128, 4, n).transpose(0, 1, 3, 2))
    if fmt == "e4m3":
        words = by_word.astype(ml_dtypes.float8_e4m3fn).view(np.uint8)
    else:
        c = by_word.astype(ml_dtypes.float4_e2m1fn).view(np.uint8) & 0xF
        words = c[..., 0::2] | (c[..., 1::2] << 4)
    return np.ascontiguousarray(words), np.ascontiguousarray(byte.astype(np.uint8).reshape(k // 512, 16, n))


def unpack_weight(words, scales, fmt):
    g, p, n, _ = words.shape
    if fmt == "e4m3":
        vals = np.ascontiguousarray(words).view(ml_dtypes.float8_e4m3fn).astype(np.float64)
    else:
        nib = np.empty((g, p, n, 4), np.uint8)
        nib[..., 0::2] = words & 0xF
        nib[..., 1::2] = words >> 4
        vals = E2M1[nib]
    vals = vals * np.repeat(np.exp2(scales.astype(np.float64) - 127.0), 8, axis=1)[..., None]
    return vals.transpose(0, 1, 3, 2).reshape(g * 512, n)

def pack4(w):
    words, scales = pack_weight(w, "e2m1")
    return words.reshape(words.shape[0], 128, -1), scales


def unpack4(words, scales):
    return unpack_weight(words.reshape(words.shape[0], 128, -1, 2), scales, "e2m1")


B, S, C, E, H = 4, 2048, 1024, 128, 16
ROPE_BASE = 10000.0
NORM_EPS = 1e-12
INV_FREQ = ROPE_BASE ** (-(np.arange(0, E, 2) / E))
THETA = S * np.repeat(INV_FREQ, 2)
SIN, COS = np.sin(THETA), np.cos(THETA)


def rotate(t):
    t1 = t[..., :-1:2]
    t2 = t[..., 1::2]
    t_rot = np.concatenate((-t2, t1), axis=-1)
    return t * COS + t_rot * SIN


def l2_normalize(t):
    n = np.sqrt((t * t).sum(-1, keepdims=True))
    return t / np.maximum(n, NORM_EPS)


def setup_inputs():
    s = mx_kscale(C)
    x = bf(np.random.standard_normal((B, S, C)) * s)
    w = np.random.standard_normal((3 * E, C)) / np.sqrt(C) / s
    words, scales = pack4(np.ascontiguousarray(w.T))
    bqkv = bf(np.random.standard_normal(3 * E) * 0.3)
    return {"x": x, "Wqkv_words": words, "Wqkv_scales": scales, "bqkv": bqkv}


def reference(x, Wqkv_words, Wqkv_scales, bqkv):
    xq = mxq(f64(x), 2, "e4m3")
    wq = unpack4(Wqkv_words, Wqkv_scales).T
    b = f64(bqkv)
    q = (xq @ wq[:E].T) + b[:E]
    k = (xq @ wq[E:2 * E].T) + b[E:2 * E]
    v = (xq @ wq[2 * E:].T) + b[2 * E:]
    return l2_normalize(rotate(q)), l2_normalize(rotate(k)), v

@@ -1,0 +1,289 @@
+from contextlib import ExitStack
+
+import concourse.mybir as mybir
+from concourse.masks import make_identity
+
+F32 = mybir.dt.float32
+BF16 = mybir.dt.bfloat16
+I32 = mybir.dt.int32
+U8 = mybir.dt.uint8
+U32 = mybir.dt.uint32
+FP8X4 = mybir.dt.float8_e4m3fn_x4
+FP4X4 = mybir.dt.float4_e2m1fn_x4
+ACT = mybir.ActivationFunctionType
+ALU = mybir.AluOpType
+AXIS = mybir.AxisListType
+
+P = 128
+TOKENS = 4 * 2048
+K = 1024
+E = 128
+PASSES = K // 512
+TILES = 4
+GROUP = TILES * P
+GROUPS = TOKENS // GROUP
+NORM_EPS = 1e-12
+THETA = [2048.0 * 10000.0 ** (-(2 * m / E)) for m in range(E // 2)]
+
+TWO_PI = 6.283185307179586
+
+FLOPS = 2 * TOKENS * K * 3 * E
+
+
+def cos_sin(angle):
+    rest = angle - round(angle / TWO_PI) * TWO_PI
+    sums = [0.0, 0.0]
+    term = 1.0
+    for n in range(32):
+        sums[n % 2] += term if n % 4 < 2 else -term
+        term *= rest / (n + 1)
+    return sums[0], sums[1]
+
+
+def tile_multiheadattention_pa_t_kernel(
+    tc, x, Wqkv_words, Wqkv_scales, bqkv, out_0, out_1, out_2
+):
+    nc = tc.nc
+    x_rows = x.flatten_outer_dims()
+    out_rows = {
+        "q": out_0.flatten_outer_dims(),
+        "k": out_1.flatten_outer_dims(),
+        "v": out_2.flatten_outer_dims(),
+    }
+
+    with ExitStack() as stack:
+        const = stack.enter_context(tc.tile_pool(name="const", bufs=1))
+        x_pool = stack.enter_context(tc.tile_pool(name="x", bufs=4))
+        mx_pool = stack.enter_context(tc.tile_pool(name="mx", bufs=2))
+        term_pool = stack.enter_context(tc.tile_pool(name="term", bufs=2))
+        norm_pool = stack.enter_context(tc.tile_pool(name="norm", bufs=2))
+        out_pool = stack.enter_context(tc.tile_pool(name="out", bufs=3))
+        xt_pool = stack.enter_context(tc.psum_pool(name="xt", bufs=3))
+        acc_pool = stack.enter_context(tc.psum_pool(name="acc", bufs=1))
+        stack.enter_context(tc.manual_schedule())
+
+        x_of, grouped_of, codes_of, xscale_of = {}, {}, {}, {}
+        product_of, terms_of, mixed_of, sums_of, norm_of = {}, {}, {}, {}, {}
+
+        def group_rows(rows, g):
+            return rows[g * GROUP : (g + 1) * GROUP, :].rearrange("(p j) w -> p j w", j=TILES)
+
+        def load_x(g, pieces):
+            x_sb = x_pool.tile([P, TILES, K], BF16, name="x_sb")
+            step = TILES // pieces
+            for j in range(0, TILES, step):
+                nc.sync.dma_start(out=x_sb[:, j : j + step, :], in_=group_rows(x_rows, g)[:, j : j + step, :])
+            x_of[g] = x_sb
+
+        load_x(0, TILES)
+
+        w_words = const.tile([P, PASSES, 3 * E * 2], U8, name="w_words", align_bytes=64)
+        for c in range(PASSES):
+            nc.sync.dma_start(out=w_words[:, c, :].bitcast(I32), in_=Wqkv_words[c].bitcast(I32))
+        w_scales = const.tile([P, PASSES, 3 * E], U8, name="w_scales", align_bytes=64)
+        nc.vector.memset(w_scales[:].rearrange("p c n -> p (c n)").bitcast(I32), 0)
+        for quadrant in range(4):
+            nc.sync.dma_start(
+                out=w_scales[32 * quadrant : 32 * quadrant + 4, :, :].bitcast(I32),
+                in_=Wqkv_scales[:, 4 * quadrant : 4 * quadrant + 4, :].rearrange("c r n -> r c n").bitcast(I32),
+            )
+        load_x(1, 1)
+
+        ident = const.tile([P, P], F32, name="ident")
+        make_identity(nc, ident[:])
+        bias_rows = const.tile([P, 3 * E], BF16, name="bias_rows")
+        nc.gpsimd.dma_start(out=bias_rows[:], in_=bqkv.partition_broadcast(P))
+
+        ones = const.tile([P, 2], F32, name="ones")
+        nc.vector.memset(ones[:], 1.0)
+        tables = const.tile([P, 4, E], F32, name="tables")
+        for m in range(E // 2):
+            nc.vector.tensor_scalar(
+                out=tables[:, 0, 2 * m : 2 * m + 2], in0=ones[:], scalar1=cos_sin(THETA[m])[0], scalar2=None, op0=ALU.mult
+            )
+        for m in range(E // 4):
+            nc.scalar.mul(out=tables[:, 1, 4 * m + 1 : 4 * m + 4 : 2], in_=ones[:], mul=-cos_sin(THETA[m])[1])
+            nc.scalar.mul(out=tables[:, 1, 4 * m : 4 * m + 3 : 2], in_=ones[:], mul=cos_sin(THETA[E // 4 + m])[1])
+
+        perm = const.tile([P, P], F32, name="perm")
+        bias_v = const.tile([P, E], F32, name="bias_v")
+        factor = const.tile([P, 4], F32, name="factor")
+        offset = const.tile([P, 4], F32, name="offset")
+
+        def finish_tables():
+            nc.vector.tensor_copy(out=perm[:, 0 : E // 2], in_=ident[:, 1:E:2])
+            nc.vector.tensor_copy(out=perm[:, E // 2 : E], in_=ident[:, 0:E:2])
+            nc.vector.tensor_copy(out=tables[:, 2:4, :], in_=bias_rows[:, 0 : 2 * E].rearrange("p (b e) -> p b e", b=2))
+            nc.vector.tensor_copy(out=bias_v[:], in_=bias_rows[:, 2 * E : 3 * E])
+            diagonal = const.tile([P, 4, E], F32, name="diagonal")
+            nc.vector.tensor_tensor(
+                out=diagonal[:], in0=tables[:], in1=ident[:].unsqueeze(1).to_broadcast([P, 4, E]), op=ALU.mult
+            )
+            nc.vector.tensor_reduce(out=factor[:], in_=diagonal[:], axis=AXIS.X, op=ALU.add)
+            nc.vector.tensor_scalar(out=offset[:, 0:2], in0=factor[:, 0:2], scalar1=factor[:, 2:3], scalar2=None, op0=ALU.mult)
+            nc.vector.tensor_scalar(out=offset[:, 2:4], in0=factor[:, 0:2], scalar1=factor[:, 3:4], scalar2=None, op0=ALU.mult)
+
+        def transpose_tile(g, j, copy):
+            if not 0 <= g < GROUPS:
+                return
+            if j == 0:
+                grouped_of[g] = mx_pool.tile([P, PASSES, GROUP, 4], BF16, name="grouped", align_bytes=64)
+            words = x_of[g][:, j, :].bitcast(F32)
+            xt = xt_pool.tile([P, PASSES * 2, P], F32, name="xt")
+            for c in range(PASSES):
+                for u in range(2):
+                    nc.tensor.transpose(xt[:, 2 * c + u, :], words[:, 256 * c + u : 256 * (c + 1) : 2], ident[:])
+            copy(
+                out=grouped_of[g][:, :, j * P : (j + 1) * P, :].bitcast(F32),
+                in_=xt[:].rearrange("p (c u) r -> p c r u", u=2),
+            )
+
+        def quantise(g):
+            if not 0 <= g < GROUPS:
+                return
+            codes = mx_pool.tile([P, PASSES, GROUP], U32, name="codes", align_bytes=64)
+            xscale = mx_pool.tile([P, PASSES, GROUP], U8, name="xscale", align_bytes=64)
+            nc.vector.quantize_mx(
+                out=codes[:].rearrange("p c r -> p (c r)").bitcast(FP8X4),
+                scales=xscale[:].rearrange("p c r -> p (c r)"),
+                in_=grouped_of[g][:].rearrange("p c r t -> p (c r t)"),
+            )
+            codes_of[g], xscale_of[g] = codes, xscale
+
+        def weight(c, n):
+            return w_words[:, c, 2 * E * n : 2 * E * (n + 1)].bitcast(FP4X4), w_scales[:, c, E * n : E * (n + 1)]
+
+        def project(g):
+            if not 0 <= g < GROUPS:
+                return
+            codes, xscale = codes_of[g], xscale_of[g]
+            for n, name in enumerate(("q", "k")):
+                product = acc_pool.tile([P, GROUP], F32, name="product_" + name)
+                for c in range(PASSES):
+                    w_c, w_scale_c = weight(c, n)
+                    nc.tensor.matmul_mx(
+                        out=product[:],
+                        lhsT=w_c,
+                        lhsT_scale=w_scale_c,
+                        rhs=codes[:, c, :].bitcast(FP8X4),
+                        rhs_scale=xscale[:, c, :],
+                        start=(c == 0),
+                        stop=(c == PASSES - 1),
+                    )
+                product_of[name, g] = product
+            product = acc_pool.tile([P, TILES, E], F32, name="product_v")
+            for j in range(TILES):
+                for c in range(PASSES):
+                    w_c, w_scale_c = weight(c, 2)
+                    nc.tensor.matmul_mx(
+                        out=product[:, j, :],
+                        lhsT=codes[:, c, j * P : (j + 1) * P].bitcast(FP8X4),
+                        lhsT_scale=xscale[:, c, j * P : (j + 1) * P],
+                        rhs=w_c,
+                        rhs_scale=w_scale_c,
+                        start=(c == 0),
+                        stop=(c == PASSES - 1),
+                    )
+            product_of["v", g] = product
+
+        def terms_q(g):
+            if not 0 <= g < GROUPS:
+                return
+            first = term_pool.tile([P, GROUP], F32, name="first_q")
+            second = term_pool.tile([P, GROUP], F32, name="second_q")
+            for i, term in enumerate((first, second)):
+                nc.scalar.activation(
+                    out=term[:], in_=product_of["q", g][:], func=ACT.Identity,
+                    scale=factor[:, i : i + 1], bias=offset[:, i : i + 1],
+                )
+            terms_of["q", g] = (first, second)
+
+        def terms_k(g):
+            if not 0 <= g < GROUPS:
+                return
+            first = term_pool.tile([P, GROUP], F32, name="first_k")
+            second = term_pool.tile([P, GROUP], F32, name="second_k")
+            for i, term in enumerate((first, second)):
+                nc.vector.tensor_scalar(
+                    out=term[:], in0=product_of["k", g][:],
+                    scalar1=factor[:, i : i + 1], scalar2=offset[:, 2 + i : 3 + i], op0=ALU.mult, op1=ALU.add,
+                )
+            terms_of["k", g] = (first, second)
+
+        def store(name, g, tile):
+            nc.sync.dma_start(out=group_rows(out_rows[name], g), in_=tile[:])
+
+        def finish_v(g):
+            if not 0 <= g < GROUPS:
+                return
+            v_sb = out_pool.tile([P, TILES, E], F32, name="v_sb")
+            nc.vector.tensor_tensor(
+                out=v_sb[:], in0=product_of["v", g][:], in1=bias_v[:].unsqueeze(1).to_broadcast([P, TILES, E]), op=ALU.add
+            )
+            store("v", g, v_sb)
+
+        def mix(g):
+            if not 0 <= g < GROUPS:
+                return
+            for name in ("q", "k"):
+                first, second = terms_of[name, g]
+                mixed = acc_pool.tile([P, TILES, E], F32, name="mixed_" + name)
+                for j in range(TILES):
+                    tokens = slice(j * P, (j + 1) * P)
+                    nc.tensor.matmul(mixed[:, j, :], lhsT=first[:, tokens], rhs=ident[:], is_transpose=True, start=True, stop=False)
+                    nc.tensor.matmul(mixed[:, j, :], lhsT=second[:, tokens], rhs=perm[:], is_transpose=True, start=False, stop=True)
+                mixed_of[name, g] = mixed
+
+        def square_sums(g, name):
+            if not 0 <= g < GROUPS:
+                return
+            if name == "q":
+                sums_of[g] = norm_pool.tile([P, 2 * TILES], F32, name="sums")
+            first_column = 0 if name == "q" else TILES
+            squares = norm_pool.tile([P, TILES, E], F32, name="squares_" + name)
+            for j in range(TILES):
+                nc.scalar.activation(
+                    out=squares[:, j, :], in_=mixed_of[name, g][:, j, :], func=ACT.Square,
+                    accum_out=sums_of[g][:, first_column + j : first_column + j + 1],
+                )
+
+        def norms(g):
+            if not 0 <= g < GROUPS:
+                return
+            norm = norm_pool.tile([P, 2 * TILES], F32, name="norm")
+            nc.scalar.activation(out=norm[:], in_=sums_of[g][:], func=ACT.Sqrt)
+            norm_of[g] = norm
+
+        def normalise(g):
+            if not 0 <= g < GROUPS:
+                return
+            rnorm = norm_pool.tile([P, 2 * TILES], F32, name="rnorm")
+            nc.vector.tensor_scalar_max(out=rnorm[:], in0=norm_of[g][:], scalar1=NORM_EPS)
+            nc.vector.reciprocal(out=rnorm[:], in_=rnorm[:])
+            for n, name in enumerate(("q", "k")):
+                unit = out_pool.tile([P, TILES, E], F32, name="unit_" + name)
+                nc.vector.tensor_tensor(
+                    out=unit[:], in0=mixed_of[name, g][:],
+                    in1=rnorm[:, n * TILES : (n + 1) * TILES].unsqueeze(2).to_broadcast([P, TILES, E]), op=ALU.mult,
+                )
+                store(name, g, unit)
+
+        for r in range(-1, GROUPS + 2):
+            if 2 <= r + 3 < GROUPS:
+                load_x(r + 3, 1)
+            square_sums(r - 2, "q")
+            terms_k(r - 1)
+            finish_v(r - 1)
+            transpose_tile(r + 1, 0, nc.scalar.copy)
+            square_sums(r - 2, "k")
+            norms(r - 2)
+            transpose_tile(r + 1, 1, nc.scalar.copy)
+            transpose_tile(r + 1, 2, nc.scalar.copy)
+            transpose_tile(r + 1, 3, nc.vector.tensor_copy)
+            normalise(r - 2)
+            quantise(r + 1)
+            if r == -1:
+                finish_tables()
+            project(r)
+            terms_q(r)
+            mix(r - 1)

@@ -107,8 +107,7 @@ def tile_multiheadattention_pa_t_kernel(
 
         perm = const.tile([P, P], F32, name="perm")
         bias_v = const.tile([P, E], F32, name="bias_v")
-        factor = const.tile([P, 4], F32, name="factor")
-        offset = const.tile([P, 4], F32, name="offset")
+        column = const.tile([P, 4], F32, name="column")
 
         def finish_tables():
             nc.vector.tensor_copy(out=perm[:, 0 : E // 2], in_=ident[:, 1:E:2])
@@ -119,11 +118,9 @@ def tile_multiheadattention_pa_t_kernel(
             nc.vector.tensor_tensor(
                 out=diagonal[:], in0=tables[:], in1=ident[:].unsqueeze(1).to_broadcast([P, 4, E]), op=ALU.mult
             )
-            nc.vector.tensor_reduce(out=factor[:], in_=diagonal[:], axis=AXIS.X, op=ALU.add)
-            nc.vector.tensor_scalar(out=offset[:, 0:2], in0=factor[:, 0:2], scalar1=factor[:, 2:3], scalar2=None, op0=ALU.mult)
-            nc.vector.tensor_scalar(out=offset[:, 2:4], in0=factor[:, 0:2], scalar1=factor[:, 3:4], scalar2=None, op0=ALU.mult)
+            nc.vector.tensor_reduce(out=column[:], in_=diagonal[:], axis=AXIS.X, op=ALU.add)
 
-        def transpose_tile(g, j, copy):
+        def transpose_tile(g, j):
             if not 0 <= g < GROUPS:
                 return
             if j == 0:
@@ -133,7 +130,7 @@ def tile_multiheadattention_pa_t_kernel(
             for c in range(PASSES):
                 for u in range(2):
                     nc.tensor.transpose(xt[:, 2 * c + u, :], words[:, 256 * c + u : 256 * (c + 1) : 2], ident[:])
-            copy(
+            nc.scalar.copy(
                 out=grouped_of[g][:, :, j * P : (j + 1) * P, :].bitcast(F32),
                 in_=xt[:].rearrange("p (c u) r -> p c r u", u=2),
             )
@@ -153,7 +150,7 @@ def tile_multiheadattention_pa_t_kernel(
         def weight(c, n):
             return w_words[:, c, 2 * E * n : 2 * E * (n + 1)].bitcast(FP4X4), w_scales[:, c, E * n : E * (n + 1)]
 
-        def project(g):
+        def project_qk(g):
             if not 0 <= g < GROUPS:
                 return
             codes, xscale = codes_of[g], xscale_of[g]
@@ -171,6 +168,11 @@ def tile_multiheadattention_pa_t_kernel(
                         stop=(c == PASSES - 1),
                     )
                 product_of[name, g] = product
+
+        def project_v(g):
+            if not 0 <= g < GROUPS:
+                return
+            codes, xscale = codes_of[g], xscale_of[g]
             product = acc_pool.tile([P, TILES, E], F32, name="product_v")
             for j in range(TILES):
                 for c in range(PASSES):
@@ -186,29 +188,20 @@ def tile_multiheadattention_pa_t_kernel(
                     )
             product_of["v", g] = product
 
-        def terms_q(g):
+        def terms(g):
             if not 0 <= g < GROUPS:
                 return
-            first = term_pool.tile([P, GROUP], F32, name="first_q")
-            second = term_pool.tile([P, GROUP], F32, name="second_q")
-            for i, term in enumerate((first, second)):
-                nc.scalar.activation(
-                    out=term[:], in_=product_of["q", g][:], func=ACT.Identity,
-                    scale=factor[:, i : i + 1], bias=offset[:, i : i + 1],
-                )
-            terms_of["q", g] = (first, second)
-
-        def terms_k(g):
-            if not 0 <= g < GROUPS:
-                return
-            first = term_pool.tile([P, GROUP], F32, name="first_k")
-            second = term_pool.tile([P, GROUP], F32, name="second_k")
-            for i, term in enumerate((first, second)):
-                nc.vector.tensor_scalar(
-                    out=term[:], in0=product_of["k", g][:],
-                    scalar1=factor[:, i : i + 1], scalar2=offset[:, 2 + i : 3 + i], op0=ALU.mult, op1=ALU.add,
-                )
-            terms_of["k", g] = (first, second)
+            for n, name in enumerate(("q", "k")):
+                raw = term_pool.tile([P, GROUP], F32, name="raw_" + name)
+                nc.vector.tensor_copy(out=raw[:], in_=product_of[name, g][:])
+                first = term_pool.tile([P, GROUP], F32, name="first_" + name)
+                second = term_pool.tile([P, GROUP], F32, name="second_" + name)
+                for i, term in enumerate((first, second)):
+                    nc.gpsimd.tensor_scalar(
+                        out=term[:], in0=raw[:], scalar1=column[:, 2 + n : 3 + n], scalar2=column[:, i : i + 1],
+                        op0=ALU.add, op1=ALU.mult,
+                    )
+                terms_of[name, g] = (first, second)
 
         def store(name, g, tile):
             nc.sync.dma_start(out=group_rows(out_rows[name], g), in_=tile[:])
@@ -272,18 +265,17 @@ def tile_multiheadattention_pa_t_kernel(
             if 2 <= r + 3 < GROUPS:
                 load_x(r + 3, 1)
             square_sums(r - 2, "q")
-            terms_k(r - 1)
-            finish_v(r - 1)
-            transpose_tile(r + 1, 0, nc.scalar.copy)
             square_sums(r - 2, "k")
             norms(r - 2)
-            transpose_tile(r + 1, 1, nc.scalar.copy)
-            transpose_tile(r + 1, 2, nc.scalar.copy)
-            transpose_tile(r + 1, 3, nc.vector.tensor_copy)
+            for j in range(TILES - 1):
+                transpose_tile(r + 1, j)
             normalise(r - 2)
+            project_qk(r)
+            terms(r)
+            transpose_tile(r + 1, TILES - 1)
             quantise(r + 1)
+            mix(r - 1)
+            project_v(r)
+            finish_v(r)
             if r == -1:
                 finish_tables()
-            project(r)
-            terms_q(r)
-            mix(r - 1)

@@ -108,6 +108,7 @@ def tile_multiheadattention_pa_t_kernel(
         perm = const.tile([P, P], F32, name="perm")
         bias_v = const.tile([P, E], F32, name="bias_v")
         column = const.tile([P, 4], F32, name="column")
+        factor_bk = const.tile([P, 1], F32, name="factor_bk")
 
         def finish_tables():
             nc.vector.tensor_copy(out=perm[:, 0 : E // 2], in_=ident[:, 1:E:2])
@@ -119,6 +120,7 @@ def tile_multiheadattention_pa_t_kernel(
                 out=diagonal[:], in0=tables[:], in1=ident[:].unsqueeze(1).to_broadcast([P, 4, E]), op=ALU.mult
             )
             nc.vector.tensor_reduce(out=column[:], in_=diagonal[:], axis=AXIS.X, op=ALU.add)
+            nc.vector.tensor_tensor(out=factor_bk[:], in0=column[:, 1:2], in1=column[:, 3:4], op=ALU.mult)
 
         def transpose_tile(g, j):
             if not 0 <= g < GROUPS:
@@ -192,13 +194,17 @@ def tile_multiheadattention_pa_t_kernel(
             if not 0 <= g < GROUPS:
                 return
             for n, name in enumerate(("q", "k")):
-                raw = term_pool.tile([P, GROUP], F32, name="raw_" + name)
-                nc.vector.tensor_copy(out=raw[:], in_=product_of[name, g][:])
                 first = term_pool.tile([P, GROUP], F32, name="first_" + name)
                 second = term_pool.tile([P, GROUP], F32, name="second_" + name)
+                if name == "k":
+                    nc.scalar.activation(
+                        out=second[:], in_=product_of[name, g][:], func=ACT.Identity, scale=column[:, 1:2], bias=factor_bk[:]
+                    )
                 for i, term in enumerate((first, second)):
-                    nc.gpsimd.tensor_scalar(
-                        out=term[:], in0=raw[:], scalar1=column[:, 2 + n : 3 + n], scalar2=column[:, i : i + 1],
+                    if name == "k" and i == 1:
+                        continue
+                    nc.vector.tensor_scalar(
+                        out=term[:], in0=product_of[name, g][:], scalar1=column[:, 2 + n : 3 + n], scalar2=column[:, i : i + 1],
                         op0=ALU.add, op1=ALU.mult,
                     )
                 terms_of[name, g] = (first, second)
@@ -264,18 +270,18 @@ def tile_multiheadattention_pa_t_kernel(
         for r in range(-1, GROUPS + 2):
             if 2 <= r + 3 < GROUPS:
                 load_x(r + 3, 1)
-            square_sums(r - 2, "q")
-            square_sums(r - 2, "k")
-            norms(r - 2)
             for j in range(TILES - 1):
                 transpose_tile(r + 1, j)
             normalise(r - 2)
+            finish_v(r - 1)
             project_qk(r)
             terms(r)
             transpose_tile(r + 1, TILES - 1)
             quantise(r + 1)
             mix(r - 1)
+            square_sums(r - 1, "q")
+            square_sums(r - 1, "k")
+            norms(r - 1)
             project_v(r)
-            finish_v(r)
             if r == -1:
                 finish_tables()

@@ -50,20 +50,24 @@ def tile_multiheadattention_pa_t_kernel(
         "k": out_1.flatten_outer_dims(),
         "v": out_2.flatten_outer_dims(),
     }
+    HALF = E // 2
 
     with ExitStack() as stack:
         const = stack.enter_context(tc.tile_pool(name="const", bufs=1))
         x_pool = stack.enter_context(tc.tile_pool(name="x", bufs=4))
-        mx_pool = stack.enter_context(tc.tile_pool(name="mx", bufs=2))
+        grouped_pool = stack.enter_context(tc.tile_pool(name="grouped", bufs=2))
+        mx_pool = stack.enter_context(tc.tile_pool(name="mx", bufs=3))
         term_pool = stack.enter_context(tc.tile_pool(name="term", bufs=2))
+        mixed_k_pool = stack.enter_context(tc.tile_pool(name="mixed_k", bufs=4))
         norm_pool = stack.enter_context(tc.tile_pool(name="norm", bufs=2))
         out_pool = stack.enter_context(tc.tile_pool(name="out", bufs=3))
         xt_pool = stack.enter_context(tc.psum_pool(name="xt", bufs=3))
         acc_pool = stack.enter_context(tc.psum_pool(name="acc", bufs=1))
+        mixed_q_pool = stack.enter_context(tc.psum_pool(name="mixed_q", bufs=2))
         stack.enter_context(tc.manual_schedule())
 
         x_of, grouped_of, codes_of, xscale_of = {}, {}, {}, {}
-        product_of, terms_of, mixed_of, sums_of, norm_of = {}, {}, {}, {}, {}
+        product_of, terms_of, mixed_of, norm_of, rnorm_of = {}, {}, {}, {}, {}
 
         def group_rows(rows, g):
             return rows[g * GROUP : (g + 1) * GROUP, :].rearrange("(p j) w -> p j w", j=TILES)
@@ -87,7 +91,7 @@ def tile_multiheadattention_pa_t_kernel(
                 out=w_scales[32 * quadrant : 32 * quadrant + 4, :, :].bitcast(I32),
                 in_=Wqkv_scales[:, 4 * quadrant : 4 * quadrant + 4, :].rearrange("c r n -> r c n").bitcast(I32),
             )
-        load_x(1, 1)
+        load_x(1, TILES)
 
         ident = const.tile([P, P], F32, name="ident")
         make_identity(nc, ident[:])
@@ -96,7 +100,7 @@ def tile_multiheadattention_pa_t_kernel(
 
         ones = const.tile([P, 2], F32, name="ones")
         nc.vector.memset(ones[:], 1.0)
-        tables = const.tile([P, 4, E], F32, name="tables")
+        tables = const.tile([P, 3, E], F32, name="tables")
         for m in range(E // 2):
             nc.vector.tensor_scalar(
                 out=tables[:, 0, 2 * m : 2 * m + 2], in0=ones[:], scalar1=cos_sin(THETA[m])[0], scalar2=None, op0=ALU.mult
@@ -106,27 +110,42 @@ def tile_multiheadattention_pa_t_kernel(
             nc.scalar.mul(out=tables[:, 1, 4 * m : 4 * m + 3 : 2], in_=ones[:], mul=cos_sin(THETA[E // 4 + m])[1])
 
         perm = const.tile([P, P], F32, name="perm")
+        bias_k = const.tile([P, E], F32, name="bias_k")
         bias_v = const.tile([P, E], F32, name="bias_v")
-        column = const.tile([P, 4], F32, name="column")
-        factor_bk = const.tile([P, 1], F32, name="factor_bk")
+        column = const.tile([P, 3], F32, name="column")
+        cos_bq = const.tile([P, 1], F32, name="cos_bq")
+        s_row = const.tile([P, E], F32, name="s_row")
+        c_row = const.tile([P, E], F32, name="c_row")
+        cos_row = tables[:, 0, :]
 
         def finish_tables():
-            nc.vector.tensor_copy(out=perm[:, 0 : E // 2], in_=ident[:, 1:E:2])
-            nc.vector.tensor_copy(out=perm[:, E // 2 : E], in_=ident[:, 0:E:2])
-            nc.vector.tensor_copy(out=tables[:, 2:4, :], in_=bias_rows[:, 0 : 2 * E].rearrange("p (b e) -> p b e", b=2))
+            nc.vector.tensor_copy(out=perm[:, 0:HALF], in_=ident[:, 1:E:2])
+            nc.vector.tensor_copy(out=perm[:, HALF:E], in_=ident[:, 0:E:2])
+            nc.vector.tensor_copy(out=tables[:, 2, :], in_=bias_rows[:, 0:E])
+            nc.vector.tensor_copy(out=bias_k[:], in_=bias_rows[:, E : 2 * E])
             nc.vector.tensor_copy(out=bias_v[:], in_=bias_rows[:, 2 * E : 3 * E])
-            diagonal = const.tile([P, 4, E], F32, name="diagonal")
+            diagonal = const.tile([P, 3, E], F32, name="diagonal")
             nc.vector.tensor_tensor(
-                out=diagonal[:], in0=tables[:], in1=ident[:].unsqueeze(1).to_broadcast([P, 4, E]), op=ALU.mult
+                out=diagonal[:], in0=tables[:], in1=ident[:].unsqueeze(1).to_broadcast([P, 3, E]), op=ALU.mult
             )
             nc.vector.tensor_reduce(out=column[:], in_=diagonal[:], axis=AXIS.X, op=ALU.add)
-            nc.vector.tensor_tensor(out=factor_bk[:], in0=column[:, 1:2], in1=column[:, 3:4], op=ALU.mult)
+            nc.vector.tensor_tensor(out=cos_bq[:], in0=column[:, 0:1], in1=column[:, 2:3], op=ALU.mult)
+            nc.vector.tensor_copy(out=s_row[:, 0:HALF], in_=tables[:, 1, 1:E:2])
+            nc.vector.tensor_copy(out=s_row[:, HALF:E], in_=tables[:, 1, 0:E:2])
+            turned = const.tile([P, E], F32, name="turned")
+            nc.vector.tensor_tensor(out=turned[:, 0:HALF], in0=bias_k[:, 1:E:2], in1=s_row[:, 0:HALF], op=ALU.mult)
+            nc.vector.tensor_tensor(out=turned[:, HALF:E], in0=bias_k[:, 0:E:2], in1=s_row[:, HALF:E], op=ALU.mult)
+            nc.vector.tensor_tensor(out=c_row[:], in0=bias_k[:], in1=cos_row, op=ALU.mult)
+            nc.vector.tensor_tensor(out=c_row[:], in0=c_row[:], in1=turned[:], op=ALU.add)
+
+        def over_tiles(row):
+            return row.unsqueeze(1).to_broadcast([P, TILES, row.shape[1]])
 
         def transpose_tile(g, j):
             if not 0 <= g < GROUPS:
                 return
             if j == 0:
-                grouped_of[g] = mx_pool.tile([P, PASSES, GROUP, 4], BF16, name="grouped", align_bytes=64)
+                grouped_of[g] = grouped_pool.tile([P, PASSES, GROUP, 4], BF16, name="grouped", align_bytes=64)
             words = x_of[g][:, j, :].bitcast(F32)
             xt = xt_pool.tile([P, PASSES * 2, P], F32, name="xt")
             for c in range(PASSES):
@@ -152,62 +171,58 @@ def tile_multiheadattention_pa_t_kernel(
         def weight(c, n):
             return w_words[:, c, 2 * E * n : 2 * E * (n + 1)].bitcast(FP4X4), w_scales[:, c, E * n : E * (n + 1)]
 
-        def project_qk(g):
+        def project_q(g):
             if not 0 <= g < GROUPS:
                 return
             codes, xscale = codes_of[g], xscale_of[g]
-            for n, name in enumerate(("q", "k")):
-                product = acc_pool.tile([P, GROUP], F32, name="product_" + name)
-                for c in range(PASSES):
-                    w_c, w_scale_c = weight(c, n)
-                    nc.tensor.matmul_mx(
-                        out=product[:],
-                        lhsT=w_c,
-                        lhsT_scale=w_scale_c,
-                        rhs=codes[:, c, :].bitcast(FP8X4),
-                        rhs_scale=xscale[:, c, :],
-                        start=(c == 0),
-                        stop=(c == PASSES - 1),
-                    )
-                product_of[name, g] = product
+            product = acc_pool.tile([P, GROUP], F32, name="product_q")
+            for c in range(PASSES):
+                w_c, w_scale_c = weight(c, 0)
+                nc.tensor.matmul_mx(
+                    out=product[:],
+                    lhsT=w_c,
+                    lhsT_scale=w_scale_c,
+                    rhs=codes[:, c, :].bitcast(FP8X4),
+                    rhs_scale=xscale[:, c, :],
+                    start=(c == 0),
+                    stop=(c == PASSES - 1),
+                )
+            product_of["q", g] = product
 
-        def project_v(g):
+        def project_kv(g):
             if not 0 <= g < GROUPS:
                 return
             codes, xscale = codes_of[g], xscale_of[g]
-            product = acc_pool.tile([P, TILES, E], F32, name="product_v")
+            for name in ("k", "v"):
+                product_of[name, g] = acc_pool.tile([P, TILES, E], F32, name="product_" + name)
             for j in range(TILES):
                 for c in range(PASSES):
-                    w_c, w_scale_c = weight(c, 2)
-                    nc.tensor.matmul_mx(
-                        out=product[:, j, :],
-                        lhsT=codes[:, c, j * P : (j + 1) * P].bitcast(FP8X4),
-                        lhsT_scale=xscale[:, c, j * P : (j + 1) * P],
-                        rhs=w_c,
-                        rhs_scale=w_scale_c,
-                        start=(c == 0),
-                        stop=(c == PASSES - 1),
-                    )
-            product_of["v", g] = product
+                    for n, name in ((1, "k"), (2, "v")):
+                        w_c, w_scale_c = weight(c, n)
+                        nc.tensor.matmul_mx(
+                            out=product_of[name, g][:, j, :],
+                            lhsT=codes[:, c, j * P : (j + 1) * P].bitcast(FP8X4),
+                            lhsT_scale=xscale[:, c, j * P : (j + 1) * P],
+                            rhs=w_c,
+                            rhs_scale=w_scale_c,
+                            start=(c == 0),
+                            stop=(c == PASSES - 1),
+                        )
 
-        def terms(g):
+        def term_q(g, i):
             if not 0 <= g < GROUPS:
                 return
-            for n, name in enumerate(("q", "k")):
-                first = term_pool.tile([P, GROUP], F32, name="first_" + name)
-                second = term_pool.tile([P, GROUP], F32, name="second_" + name)
-                if name == "k":
-                    nc.scalar.activation(
-                        out=second[:], in_=product_of[name, g][:], func=ACT.Identity, scale=column[:, 1:2], bias=factor_bk[:]
-                    )
-                for i, term in enumerate((first, second)):
-                    if name == "k" and i == 1:
-                        continue
-                    nc.vector.tensor_scalar(
-                        out=term[:], in0=product_of[name, g][:], scalar1=column[:, 2 + n : 3 + n], scalar2=column[:, i : i + 1],
-                        op0=ALU.add, op1=ALU.mult,
-                    )
-                terms_of[name, g] = (first, second)
+            made = term_pool.tile([P, GROUP], F32, name=("first_q", "second_q")[i])
+            if i == 0:
+                nc.scalar.activation(
+                    out=made[:], in_=product_of["q", g][:], func=ACT.Identity, scale=column[:, 0:1], bias=cos_bq[:]
+                )
+            else:
+                nc.vector.tensor_scalar(
+                    out=made[:], in0=product_of["q", g][:], scalar1=column[:, 2:3], scalar2=column[:, 1:2],
+                    op0=ALU.add, op1=ALU.mult,
+                )
+            terms_of["q", i, g] = made
 
         def store(name, g, tile):
             nc.sync.dma_start(out=group_rows(out_rows[name], g), in_=tile[:])
@@ -216,72 +231,90 @@ def tile_multiheadattention_pa_t_kernel(
             if not 0 <= g < GROUPS:
                 return
             v_sb = out_pool.tile([P, TILES, E], F32, name="v_sb")
-            nc.vector.tensor_tensor(
-                out=v_sb[:], in0=product_of["v", g][:], in1=bias_v[:].unsqueeze(1).to_broadcast([P, TILES, E]), op=ALU.add
-            )
+            nc.vector.tensor_tensor(out=v_sb[:], in0=product_of["v", g][:], in1=over_tiles(bias_v[:]), op=ALU.add)
             store("v", g, v_sb)
 
-        def mix(g):
+        def mix_q(g):
             if not 0 <= g < GROUPS:
                 return
-            for name in ("q", "k"):
-                first, second = terms_of[name, g]
-                mixed = acc_pool.tile([P, TILES, E], F32, name="mixed_" + name)
-                for j in range(TILES):
-                    tokens = slice(j * P, (j + 1) * P)
-                    nc.tensor.matmul(mixed[:, j, :], lhsT=first[:, tokens], rhs=ident[:], is_transpose=True, start=True, stop=False)
-                    nc.tensor.matmul(mixed[:, j, :], lhsT=second[:, tokens], rhs=perm[:], is_transpose=True, start=False, stop=True)
-                mixed_of[name, g] = mixed
+            first, second = terms_of["q", 0, g], terms_of["q", 1, g]
+            mixed = mixed_q_pool.tile([P, TILES, E], F32, name="mixed_q")
+            for j in range(TILES):
+                tokens = slice(j * P, (j + 1) * P)
+                nc.tensor.matmul(mixed[:, j, :], lhsT=first[:, tokens], rhs=ident[:], is_transpose=True, start=True, stop=False)
+                nc.tensor.matmul(mixed[:, j, :], lhsT=second[:, tokens], rhs=perm[:], is_transpose=True, start=False, stop=True)
+            mixed_of["q", g] = mixed
 
-        def square_sums(g, name):
+        def products_k(g):
             if not 0 <= g < GROUPS:
                 return
-            if name == "q":
-                sums_of[g] = norm_pool.tile([P, 2 * TILES], F32, name="sums")
-            first_column = 0 if name == "q" else TILES
+            product = product_of["k", g]
+            straight = term_pool.tile([P, TILES, E], F32, name="straight_k")
+            turned = term_pool.tile([P, TILES, E], F32, name="turned_k")
+            nc.vector.tensor_tensor(out=straight[:], in0=product[:], in1=over_tiles(cos_row), op=ALU.mult)
+            nc.vector.tensor_tensor(out=turned[:, :, 0:HALF], in0=product[:, :, 1:E:2], in1=over_tiles(s_row[:, 0:HALF]), op=ALU.mult)
+            nc.vector.tensor_tensor(out=turned[:, :, HALF:E], in0=product[:, :, 0:E:2], in1=over_tiles(s_row[:, HALF:E]), op=ALU.mult)
+            terms_of["k", g] = (straight, turned)
+
+        def mix_k(g):
+            if not 0 <= g < GROUPS:
+                return
+            straight, turned = terms_of["k", g]
+            mixed = mixed_k_pool.tile([P, TILES, E], F32, name="mixed_k")
+            nc.gpsimd.tensor_tensor(out=mixed[:], in0=straight[:], in1=turned[:], op=ALU.add)
+            nc.gpsimd.tensor_tensor(out=mixed[:], in0=mixed[:], in1=over_tiles(c_row[:]), op=ALU.add)
+            mixed_of["k", g] = mixed
+
+        def norms(g, name):
+            if not 0 <= g < GROUPS:
+                return
+            sums = norm_pool.tile([P, TILES], F32, name="sums_" + name)
             squares = norm_pool.tile([P, TILES, E], F32, name="squares_" + name)
             for j in range(TILES):
                 nc.scalar.activation(
-                    out=squares[:, j, :], in_=mixed_of[name, g][:, j, :], func=ACT.Square,
-                    accum_out=sums_of[g][:, first_column + j : first_column + j + 1],
+                    out=squares[:, j, :], in_=mixed_of[name, g][:, j, :], func=ACT.Square, accum_out=sums[:, j : j + 1]
                 )
+            norm = norm_pool.tile([P, TILES], F32, name="norm_" + name)
+            nc.scalar.activation(out=norm[:], in_=sums[:], func=ACT.Sqrt)
+            norm_of[name, g] = norm
 
-        def norms(g):
+        def reciprocal_norms(g, name):
             if not 0 <= g < GROUPS:
                 return
-            norm = norm_pool.tile([P, 2 * TILES], F32, name="norm")
-            nc.scalar.activation(out=norm[:], in_=sums_of[g][:], func=ACT.Sqrt)
-            norm_of[g] = norm
-
-        def normalise(g):
-            if not 0 <= g < GROUPS:
-                return
-            rnorm = norm_pool.tile([P, 2 * TILES], F32, name="rnorm")
-            nc.vector.tensor_scalar_max(out=rnorm[:], in0=norm_of[g][:], scalar1=NORM_EPS)
+            rnorm = norm_pool.tile([P, TILES], F32, name="rnorm_" + name)
+            nc.vector.tensor_scalar_max(out=rnorm[:], in0=norm_of[name, g][:], scalar1=NORM_EPS)
             nc.vector.reciprocal(out=rnorm[:], in_=rnorm[:])
-            for n, name in enumerate(("q", "k")):
-                unit = out_pool.tile([P, TILES, E], F32, name="unit_" + name)
-                nc.vector.tensor_tensor(
-                    out=unit[:], in0=mixed_of[name, g][:],
-                    in1=rnorm[:, n * TILES : (n + 1) * TILES].unsqueeze(2).to_broadcast([P, TILES, E]), op=ALU.mult,
-                )
-                store(name, g, unit)
+            rnorm_of[name, g] = rnorm
 
-        for r in range(-1, GROUPS + 2):
-            if 2 <= r + 3 < GROUPS:
-                load_x(r + 3, 1)
+        def normalise(g, name):
+            if not 0 <= g < GROUPS:
+                return
+            unit = out_pool.tile([P, TILES, E], F32, name="unit_" + name)
+            nc.vector.tensor_tensor(
+                out=unit[:], in0=mixed_of[name, g][:], in1=rnorm_of[name, g][:].unsqueeze(2).to_broadcast([P, TILES, E]), op=ALU.mult
+            )
+            store(name, g, unit)
+
+        for r in range(-2, GROUPS + 4):
+            if 2 <= r + 4 < GROUPS:
+                load_x(r + 4, 1)
             for j in range(TILES - 1):
-                transpose_tile(r + 1, j)
-            normalise(r - 2)
+                transpose_tile(r + 2, j)
             finish_v(r - 1)
-            project_qk(r)
-            terms(r)
-            transpose_tile(r + 1, TILES - 1)
-            quantise(r + 1)
-            mix(r - 1)
-            square_sums(r - 1, "q")
-            square_sums(r - 1, "k")
-            norms(r - 1)
-            project_v(r)
-            if r == -1:
+            products_k(r - 1)
+            mix_k(r - 1)
+            project_q(r)
+            reciprocal_norms(r - 2, "q")
+            reciprocal_norms(r - 3, "k")
+            term_q(r, 0)
+            term_q(r, 1)
+            transpose_tile(r + 2, TILES - 1)
+            normalise(r - 2, "q")
+            normalise(r - 3, "k")
+            quantise(r + 2)
+            mix_q(r - 1)
+            norms(r - 1, "q")
+            norms(r - 2, "k")
+            project_kv(r)
+            if r == -2:
                 finish_tables()

@@ -51,6 +51,7 @@ def tile_multiheadattention_pa_t_kernel(
         "v": out_2.flatten_outer_dims(),
     }
     HALF = E // 2
+    SCALAR_SHARE = 20
 
     with ExitStack() as stack:
         const = stack.enter_context(tc.tile_pool(name="const", bufs=1))
@@ -79,7 +80,8 @@ def tile_multiheadattention_pa_t_kernel(
                 nc.sync.dma_start(out=x_sb[:, j : j + step, :], in_=group_rows(x_rows, g)[:, j : j + step, :])
             x_of[g] = x_sb
 
-        load_x(0, TILES)
+        for g in range(3):
+            load_x(g, TILES)
 
         w_words = const.tile([P, PASSES, 3 * E * 2], U8, name="w_words", align_bytes=64)
         for c in range(PASSES):
@@ -91,7 +93,7 @@ def tile_multiheadattention_pa_t_kernel(
                 out=w_scales[32 * quadrant : 32 * quadrant + 4, :, :].bitcast(I32),
                 in_=Wqkv_scales[:, 4 * quadrant : 4 * quadrant + 4, :].rearrange("c r n -> r c n").bitcast(I32),
             )
-        load_x(1, TILES)
+        load_x(3, 1)
 
         ident = const.tile([P, P], F32, name="ident")
         make_identity(nc, ident[:])
@@ -106,8 +108,14 @@ def tile_multiheadattention_pa_t_kernel(
                 out=tables[:, 0, 2 * m : 2 * m + 2], in0=ones[:], scalar1=cos_sin(THETA[m])[0], scalar2=None, op0=ALU.mult
             )
         for m in range(E // 4):
-            nc.scalar.mul(out=tables[:, 1, 4 * m + 1 : 4 * m + 4 : 2], in_=ones[:], mul=-cos_sin(THETA[m])[1])
-            nc.scalar.mul(out=tables[:, 1, 4 * m : 4 * m + 3 : 2], in_=ones[:], mul=cos_sin(THETA[E // 4 + m])[1])
+            for columns_of_m, factor in (
+                (slice(4 * m + 1, 4 * m + 4, 2), -cos_sin(THETA[m])[1]),
+                (slice(4 * m, 4 * m + 3, 2), cos_sin(THETA[E // 4 + m])[1]),
+            ):
+                if m < SCALAR_SHARE:
+                    nc.scalar.mul(out=tables[:, 1, columns_of_m], in_=ones[:], mul=factor)
+                else:
+                    nc.vector.tensor_scalar(out=tables[:, 1, columns_of_m], in0=ones[:], scalar1=factor, scalar2=None, op0=ALU.mult)
 
         perm = const.tile([P, P], F32, name="perm")
         bias_k = const.tile([P, E], F32, name="bias_k")
@@ -261,42 +269,54 @@ def tile_multiheadattention_pa_t_kernel(
                 return
             straight, turned = terms_of["k", g]
             mixed = mixed_k_pool.tile([P, TILES, E], F32, name="mixed_k")
-            nc.gpsimd.tensor_tensor(out=mixed[:], in0=straight[:], in1=turned[:], op=ALU.add)
-            nc.gpsimd.tensor_tensor(out=mixed[:], in0=mixed[:], in1=over_tiles(c_row[:]), op=ALU.add)
+            engine = nc.gpsimd if g < GROUPS - 1 else nc.vector
+            engine.tensor_tensor(out=mixed[:], in0=straight[:], in1=turned[:], op=ALU.add)
+            engine.tensor_tensor(out=mixed[:], in0=mixed[:], in1=over_tiles(c_row[:]), op=ALU.add)
             mixed_of["k", g] = mixed
 
-        def norms(g, name):
-            if not 0 <= g < GROUPS:
-                return
-            sums = norm_pool.tile([P, TILES], F32, name="sums_" + name)
-            squares = norm_pool.tile([P, TILES, E], F32, name="squares_" + name)
-            for j in range(TILES):
-                nc.scalar.activation(
-                    out=squares[:, j, :], in_=mixed_of[name, g][:, j, :], func=ACT.Square, accum_out=sums[:, j : j + 1]
-                )
-            norm = norm_pool.tile([P, TILES], F32, name="norm_" + name)
-            nc.scalar.activation(out=norm[:], in_=sums[:], func=ACT.Sqrt)
-            norm_of[name, g] = norm
+        def columns(g_q, g_k):
+            return slice(0 if 0 <= g_q < GROUPS else TILES, 2 * TILES if 0 <= g_k < GROUPS else TILES)
 
-        def reciprocal_norms(g, name):
-            if not 0 <= g < GROUPS:
+        def norms(g_q, g_k):
+            held = columns(g_q, g_k)
+            if held.start >= held.stop:
                 return
-            rnorm = norm_pool.tile([P, TILES], F32, name="rnorm_" + name)
-            nc.vector.tensor_scalar_max(out=rnorm[:], in0=norm_of[name, g][:], scalar1=NORM_EPS)
-            nc.vector.reciprocal(out=rnorm[:], in_=rnorm[:])
-            rnorm_of[name, g] = rnorm
+            sums = norm_pool.tile([P, 2 * TILES], F32, name="sums")
+            for n, (name, g) in enumerate((("q", g_q), ("k", g_k))):
+                if not 0 <= g < GROUPS:
+                    continue
+                squares = norm_pool.tile([P, TILES, E], F32, name="squares_" + name)
+                for j in range(TILES):
+                    nc.scalar.activation(
+                        out=squares[:, j, :], in_=mixed_of[name, g][:, j, :], func=ACT.Square,
+                        accum_out=sums[:, n * TILES + j : n * TILES + j + 1],
+                    )
+            norm = norm_pool.tile([P, 2 * TILES], F32, name="norm")
+            nc.scalar.activation(out=norm[:, held], in_=sums[:, held], func=ACT.Sqrt)
+            norm_of[g_q, g_k] = norm
+
+        def reciprocal_norms(g_q, g_k):
+            held = columns(g_q, g_k)
+            if held.start >= held.stop:
+                return
+            rnorm = norm_pool.tile([P, 2 * TILES], F32, name="rnorm")
+            nc.vector.tensor_scalar_max(out=rnorm[:, held], in0=norm_of[g_q, g_k][:, held], scalar1=NORM_EPS)
+            nc.vector.reciprocal(out=rnorm[:, held], in_=rnorm[:, held])
+            rnorm_of["q", g_q] = rnorm[:, 0:TILES]
+            rnorm_of["k", g_k] = rnorm[:, TILES : 2 * TILES]
 
         def normalise(g, name):
             if not 0 <= g < GROUPS:
                 return
             unit = out_pool.tile([P, TILES, E], F32, name="unit_" + name)
-            nc.vector.tensor_tensor(
-                out=unit[:], in0=mixed_of[name, g][:], in1=rnorm_of[name, g][:].unsqueeze(2).to_broadcast([P, TILES, E]), op=ALU.mult
+            engine = nc.vector if name == "q" or g >= GROUPS - 2 else nc.gpsimd
+            engine.tensor_tensor(
+                out=unit[:], in0=mixed_of[name, g][:], in1=rnorm_of[name, g].unsqueeze(2).to_broadcast([P, TILES, E]), op=ALU.mult
             )
             store(name, g, unit)
 
         for r in range(-2, GROUPS + 4):
-            if 2 <= r + 4 < GROUPS:
+            if 4 <= r + 4 < GROUPS:
                 load_x(r + 4, 1)
             for j in range(TILES - 1):
                 transpose_tile(r + 2, j)
@@ -304,8 +324,7 @@ def tile_multiheadattention_pa_t_kernel(
             products_k(r - 1)
             mix_k(r - 1)
             project_q(r)
-            reciprocal_norms(r - 2, "q")
-            reciprocal_norms(r - 3, "k")
+            reciprocal_norms(r - 2, r - 3)
             term_q(r, 0)
             term_q(r, 1)
             transpose_tile(r + 2, TILES - 1)
@@ -313,8 +332,7 @@ def tile_multiheadattention_pa_t_kernel(
             normalise(r - 3, "k")
             quantise(r + 2)
             mix_q(r - 1)
-            norms(r - 1, "q")
-            norms(r - 2, "k")
+            norms(r - 1, r - 2)
             project_kv(r)
             if r == -2:
                 finish_tables()

from contextlib import ExitStack

import concourse.mybir as mybir
from concourse.masks import make_identity

F32 = mybir.dt.float32
BF16 = mybir.dt.bfloat16
I32 = mybir.dt.int32
U8 = mybir.dt.uint8
U32 = mybir.dt.uint32
FP8X4 = mybir.dt.float8_e4m3fn_x4
FP4X4 = mybir.dt.float4_e2m1fn_x4
ACT = mybir.ActivationFunctionType
ALU = mybir.AluOpType
AXIS = mybir.AxisListType

P = 128
TOKENS = 4 * 2048
K = 1024
E = 128
PASSES = K // 512
TILES = 4
GROUP = TILES * P
GROUPS = TOKENS // GROUP
NORM_EPS = 1e-12
THETA = [2048.0 * 10000.0 ** (-(2 * m / E)) for m in range(E // 2)]

TWO_PI = 6.283185307179586

FLOPS = 2 * TOKENS * K * 3 * E


def cos_sin(angle):
    rest = angle - round(angle / TWO_PI) * TWO_PI
    sums = [0.0, 0.0]
    term = 1.0
    for n in range(32):
        sums[n % 2] += term if n % 4 < 2 else -term
        term *= rest / (n + 1)
    return sums[0], sums[1]


def tile_multiheadattention_pa_t_kernel(
    tc, x, Wqkv_words, Wqkv_scales, bqkv, out_0, out_1, out_2
):
    nc = tc.nc
    x_rows = x.flatten_outer_dims()
    out_rows = {
        "q": out_0.flatten_outer_dims(),
        "k": out_1.flatten_outer_dims(),
        "v": out_2.flatten_outer_dims(),
    }
    HALF = E // 2
    SCALAR_SHARE = 20

    with ExitStack() as stack:
        const = stack.enter_context(tc.tile_pool(name="const", bufs=1))
        x_pool = stack.enter_context(tc.tile_pool(name="x", bufs=4))
        grouped_pool = stack.enter_context(tc.tile_pool(name="grouped", bufs=2))
        mx_pool = stack.enter_context(tc.tile_pool(name="mx", bufs=3))
        term_pool = stack.enter_context(tc.tile_pool(name="term", bufs=2))
        mixed_k_pool = stack.enter_context(tc.tile_pool(name="mixed_k", bufs=4))
        norm_pool = stack.enter_context(tc.tile_pool(name="norm", bufs=2))
        out_pool = stack.enter_context(tc.tile_pool(name="out", bufs=3))
        xt_pool = stack.enter_context(tc.psum_pool(name="xt", bufs=3))
        acc_pool = stack.enter_context(tc.psum_pool(name="acc", bufs=1))
        mixed_q_pool = stack.enter_context(tc.psum_pool(name="mixed_q", bufs=2))
        stack.enter_context(tc.manual_schedule())

        x_of, grouped_of, codes_of, xscale_of = {}, {}, {}, {}
        product_of, terms_of, mixed_of, norm_of, rnorm_of = {}, {}, {}, {}, {}

        def group_rows(rows, g):
            return rows[g * GROUP : (g + 1) * GROUP, :].rearrange("(p j) w -> p j w", j=TILES)

        def load_x(g, pieces):
            x_sb = x_pool.tile([P, TILES, K], BF16, name="x_sb")
            step = TILES // pieces
            for j in range(0, TILES, step):
                nc.sync.dma_start(out=x_sb[:, j : j + step, :], in_=group_rows(x_rows, g)[:, j : j + step, :])
            x_of[g] = x_sb

        for g in range(3):
            load_x(g, TILES)

        w_words = const.tile([P, PASSES, 3 * E * 2], U8, name="w_words", align_bytes=64)
        for c in range(PASSES):
            nc.sync.dma_start(out=w_words[:, c, :].bitcast(I32), in_=Wqkv_words[c].bitcast(I32))
        w_scales = const.tile([P, PASSES, 3 * E], U8, name="w_scales", align_bytes=64)
        nc.vector.memset(w_scales[:].rearrange("p c n -> p (c n)").bitcast(I32), 0)
        for quadrant in range(4):
            nc.sync.dma_start(
                out=w_scales[32 * quadrant : 32 * quadrant + 4, :, :].bitcast(I32),
                in_=Wqkv_scales[:, 4 * quadrant : 4 * quadrant + 4, :].rearrange("c r n -> r c n").bitcast(I32),
            )
        load_x(3, 1)

        ident = const.tile([P, P], F32, name="ident")
        make_identity(nc, ident[:])
        bias_rows = const.tile([P, 3 * E], BF16, name="bias_rows")
        nc.gpsimd.dma_start(out=bias_rows[:], in_=bqkv.partition_broadcast(P))

        ones = const.tile([P, 2], F32, name="ones")
        nc.vector.memset(ones[:], 1.0)
        tables = const.tile([P, 3, E], F32, name="tables")
        for m in range(E // 2):
            nc.vector.tensor_scalar(
                out=tables[:, 0, 2 * m : 2 * m + 2], in0=ones[:], scalar1=cos_sin(THETA[m])[0], scalar2=None, op0=ALU.mult
            )
        for m in range(E // 4):
            for columns_of_m, factor in (
                (slice(4 * m + 1, 4 * m + 4, 2), -cos_sin(THETA[m])[1]),
                (slice(4 * m, 4 * m + 3, 2), cos_sin(THETA[E // 4 + m])[1]),
            ):
                if m < SCALAR_SHARE:
                    nc.scalar.mul(out=tables[:, 1, columns_of_m], in_=ones[:], mul=factor)
                else:
                    nc.vector.tensor_scalar(out=tables[:, 1, columns_of_m], in0=ones[:], scalar1=factor, scalar2=None, op0=ALU.mult)

        perm = const.tile([P, P], F32, name="perm")
        bias_k = const.tile([P, E], F32, name="bias_k")
        bias_v = const.tile([P, E], F32, name="bias_v")
        column = const.tile([P, 3], F32, name="column")
        cos_bq = const.tile([P, 1], F32, name="cos_bq")
        s_row = const.tile([P, E], F32, name="s_row")
        c_row = const.tile([P, E], F32, name="c_row")
        cos_row = tables[:, 0, :]

        def finish_tables():
            nc.vector.tensor_copy(out=perm[:, 0:HALF], in_=ident[:, 1:E:2])
            nc.vector.tensor_copy(out=perm[:, HALF:E], in_=ident[:, 0:E:2])
            nc.vector.tensor_copy(out=tables[:, 2, :], in_=bias_rows[:, 0:E])
            nc.vector.tensor_copy(out=bias_k[:], in_=bias_rows[:, E : 2 * E])
            nc.vector.tensor_copy(out=bias_v[:], in_=bias_rows[:, 2 * E : 3 * E])
            diagonal = const.tile([P, 3, E], F32, name="diagonal")
            nc.vector.tensor_tensor(
                out=diagonal[:], in0=tables[:], in1=ident[:].unsqueeze(1).to_broadcast([P, 3, E]), op=ALU.mult
            )
            nc.vector.tensor_reduce(out=column[:], in_=diagonal[:], axis=AXIS.X, op=ALU.add)
            nc.vector.tensor_tensor(out=cos_bq[:], in0=column[:, 0:1], in1=column[:, 2:3], op=ALU.mult)
            nc.vector.tensor_copy(out=s_row[:, 0:HALF], in_=tables[:, 1, 1:E:2])
            nc.vector.tensor_copy(out=s_row[:, HALF:E], in_=tables[:, 1, 0:E:2])
            turned = const.tile([P, E], F32, name="turned")
            nc.vector.tensor_tensor(out=turned[:, 0:HALF], in0=bias_k[:, 1:E:2], in1=s_row[:, 0:HALF], op=ALU.mult)
            nc.vector.tensor_tensor(out=turned[:, HALF:E], in0=bias_k[:, 0:E:2], in1=s_row[:, HALF:E], op=ALU.mult)
            nc.vector.tensor_tensor(out=c_row[:], in0=bias_k[:], in1=cos_row, op=ALU.mult)
            nc.vector.tensor_tensor(out=c_row[:], in0=c_row[:], in1=turned[:], op=ALU.add)

        def over_tiles(row):
            return row.unsqueeze(1).to_broadcast([P, TILES, row.shape[1]])

        def transpose_tile(g, j):
            if not 0 <= g < GROUPS:
                return
            if j == 0:
                grouped_of[g] = grouped_pool.tile([P, PASSES, GROUP, 4], BF16, name="grouped", align_bytes=64)
            words = x_of[g][:, j, :].bitcast(F32)
            xt = xt_pool.tile([P, PASSES * 2, P], F32, name="xt")
            for c in range(PASSES):
                for u in range(2):
                    nc.tensor.transpose(xt[:, 2 * c + u, :], words[:, 256 * c + u : 256 * (c + 1) : 2], ident[:])
            nc.scalar.copy(
                out=grouped_of[g][:, :, j * P : (j + 1) * P, :].bitcast(F32),
                in_=xt[:].rearrange("p (c u) r -> p c r u", u=2),
            )

        def quantise(g):
            if not 0 <= g < GROUPS:
                return
            codes = mx_pool.tile([P, PASSES, GROUP], U32, name="codes", align_bytes=64)
            xscale = mx_pool.tile([P, PASSES, GROUP], U8, name="xscale", align_bytes=64)
            nc.vector.quantize_mx(
                out=codes[:].rearrange("p c r -> p (c r)").bitcast(FP8X4),
                scales=xscale[:].rearrange("p c r -> p (c r)"),
                in_=grouped_of[g][:].rearrange("p c r t -> p (c r t)"),
            )
            codes_of[g], xscale_of[g] = codes, xscale

        def weight(c, n):
            return w_words[:, c, 2 * E * n : 2 * E * (n + 1)].bitcast(FP4X4), w_scales[:, c, E * n : E * (n + 1)]

        def project_q(g):
            if not 0 <= g < GROUPS:
                return
            codes, xscale = codes_of[g], xscale_of[g]
            product = acc_pool.tile([P, GROUP], F32, name="product_q")
            for c in range(PASSES):
                w_c, w_scale_c = weight(c, 0)
                nc.tensor.matmul_mx(
                    out=product[:],
                    lhsT=w_c,
                    lhsT_scale=w_scale_c,
                    rhs=codes[:, c, :].bitcast(FP8X4),
                    rhs_scale=xscale[:, c, :],
                    start=(c == 0),
                    stop=(c == PASSES - 1),
                )
            product_of["q", g] = product

        def project_kv(g):
            if not 0 <= g < GROUPS:
                return
            codes, xscale = codes_of[g], xscale_of[g]
            for name in ("k", "v"):
                product_of[name, g] = acc_pool.tile([P, TILES, E], F32, name="product_" + name)
            for j in range(TILES):
                for c in range(PASSES):
                    for n, name in ((1, "k"), (2, "v")):
                        w_c, w_scale_c = weight(c, n)
                        nc.tensor.matmul_mx(
                            out=product_of[name, g][:, j, :],
                            lhsT=codes[:, c, j * P : (j + 1) * P].bitcast(FP8X4),
                            lhsT_scale=xscale[:, c, j * P : (j + 1) * P],
                            rhs=w_c,
                            rhs_scale=w_scale_c,
                            start=(c == 0),
                            stop=(c == PASSES - 1),
                        )

        def term_q(g, i):
            if not 0 <= g < GROUPS:
                return
            made = term_pool.tile([P, GROUP], F32, name=("first_q", "second_q")[i])
            if i == 0:
                nc.scalar.activation(
                    out=made[:], in_=product_of["q", g][:], func=ACT.Identity, scale=column[:, 0:1], bias=cos_bq[:]
                )
            else:
                nc.vector.tensor_scalar(
                    out=made[:], in0=product_of["q", g][:], scalar1=column[:, 2:3], scalar2=column[:, 1:2],
                    op0=ALU.add, op1=ALU.mult,
                )
            terms_of["q", i, g] = made

        def store(name, g, tile):
            nc.sync.dma_start(out=group_rows(out_rows[name], g), in_=tile[:])

        def finish_v(g):
            if not 0 <= g < GROUPS:
                return
            v_sb = out_pool.tile([P, TILES, E], F32, name="v_sb")
            nc.vector.tensor_tensor(out=v_sb[:], in0=product_of["v", g][:], in1=over_tiles(bias_v[:]), op=ALU.add)
            store("v", g, v_sb)

        def mix_q(g):
            if not 0 <= g < GROUPS:
                return
            first, second = terms_of["q", 0, g], terms_of["q", 1, g]
            mixed = mixed_q_pool.tile([P, TILES, E], F32, name="mixed_q")
            for j in range(TILES):
                tokens = slice(j * P, (j + 1) * P)
                nc.tensor.matmul(mixed[:, j, :], lhsT=first[:, tokens], rhs=ident[:], is_transpose=True, start=True, stop=False)
                nc.tensor.matmul(mixed[:, j, :], lhsT=second[:, tokens], rhs=perm[:], is_transpose=True, start=False, stop=True)
            mixed_of["q", g] = mixed

        def products_k(g):
            if not 0 <= g < GROUPS:
                return
            product = product_of["k", g]
            straight = term_pool.tile([P, TILES, E], F32, name="straight_k")
            turned = term_pool.tile([P, TILES, E], F32, name="turned_k")
            nc.vector.tensor_tensor(out=straight[:], in0=product[:], in1=over_tiles(cos_row), op=ALU.mult)
            nc.vector.tensor_tensor(out=turned[:, :, 0:HALF], in0=product[:, :, 1:E:2], in1=over_tiles(s_row[:, 0:HALF]), op=ALU.mult)
            nc.vector.tensor_tensor(out=turned[:, :, HALF:E], in0=product[:, :, 0:E:2], in1=over_tiles(s_row[:, HALF:E]), op=ALU.mult)
            terms_of["k", g] = (straight, turned)

        def mix_k(g):
            if not 0 <= g < GROUPS:
                return
            straight, turned = terms_of["k", g]
            mixed = mixed_k_pool.tile([P, TILES, E], F32, name="mixed_k")
            engine = nc.gpsimd if g < GROUPS - 1 else nc.vector
            engine.tensor_tensor(out=mixed[:], in0=straight[:], in1=turned[:], op=ALU.add)
            engine.tensor_tensor(out=mixed[:], in0=mixed[:], in1=over_tiles(c_row[:]), op=ALU.add)
            mixed_of["k", g] = mixed

        def columns(g_q, g_k):
            return slice(0 if 0 <= g_q < GROUPS else TILES, 2 * TILES if 0 <= g_k < GROUPS else TILES)

        def norms(g_q, g_k):
            held = columns(g_q, g_k)
            if held.start >= held.stop:
                return
            sums = norm_pool.tile([P, 2 * TILES], F32, name="sums")
            for n, (name, g) in enumerate((("q", g_q), ("k", g_k))):
                if not 0 <= g < GROUPS:
                    continue
                squares = norm_pool.tile([P, TILES, E], F32, name="squares_" + name)
                for j in range(TILES):
                    nc.scalar.activation(
                        out=squares[:, j, :], in_=mixed_of[name, g][:, j, :], func=ACT.Square,
                        accum_out=sums[:, n * TILES + j : n * TILES + j + 1],
                    )
            norm = norm_pool.tile([P, 2 * TILES], F32, name="norm")
            nc.scalar.activation(out=norm[:, held], in_=sums[:, held], func=ACT.Sqrt)
            norm_of[g_q, g_k] = norm

        def reciprocal_norms(g_q, g_k):
            held = columns(g_q, g_k)
            if held.start >= held.stop:
                return
            rnorm = norm_pool.tile([P, 2 * TILES], F32, name="rnorm")
            nc.vector.tensor_scalar_max(out=rnorm[:, held], in0=norm_of[g_q, g_k][:, held], scalar1=NORM_EPS)
            nc.vector.reciprocal(out=rnorm[:, held], in_=rnorm[:, held])
            rnorm_of["q", g_q] = rnorm[:, 0:TILES]
            rnorm_of["k", g_k] = rnorm[:, TILES : 2 * TILES]

        def normalise(g, name):
            if not 0 <= g < GROUPS:
                return
            unit = out_pool.tile([P, TILES, E], F32, name="unit_" + name)
            engine = nc.vector if name == "q" or g >= GROUPS - 2 else nc.gpsimd
            engine.tensor_tensor(
                out=unit[:], in0=mixed_of[name, g][:], in1=rnorm_of[name, g].unsqueeze(2).to_broadcast([P, TILES, E]), op=ALU.mult
            )
            store(name, g, unit)

        for r in range(-2, GROUPS + 4):
            if 4 <= r + 4 < GROUPS:
                load_x(r + 4, 1)
            for j in range(TILES - 1):
                transpose_tile(r + 2, j)
            finish_v(r - 1)
            products_k(r - 1)
            mix_k(r - 1)
            project_q(r)
            reciprocal_norms(r - 2, r - 3)
            term_q(r, 0)
            term_q(r, 1)
            transpose_tile(r + 2, TILES - 1)
            normalise(r - 2, "q")
            normalise(r - 3, "k")
            quantise(r + 2)
            mix_q(r - 1)
            norms(r - 1, r - 2)
            project_kv(r)
            if r == -2:
                finish_tables()
